import numpy as np
import ml_dtypes


def mxq(x, axis, fmt="e4m3"):
    dtype, down = {"e4m3": (ml_dtypes.float8_e4m3fn, 7), "e5m2": (ml_dtypes.float8_e5m2, 14)}[fmt]
    v = np.moveaxis(np.asarray(x, np.float32).astype(ml_dtypes.bfloat16).astype(np.float64), axis, -1)
    blocks = v.reshape(v.shape[:-1] + (-1, 32))
    amax = np.abs(blocks).max(-1, keepdims=True)
    byte = np.maximum(np.where(amax > 0, np.frexp(amax)[1] - 1 + 127, 0) - down, 1)
    scale = np.exp2(byte - 127.0)
    codes = (blocks / scale).astype(np.float32).astype(dtype).astype(np.float64)
    return np.moveaxis((codes * scale).reshape(v.shape), -1, axis)


WIDE = False


def mx_kscale(k):
    if not WIDE:
        return np.ones(k)
    levels = np.array([30, -30])
    if k % 512:
        return np.exp2(np.random.permutation(np.resize(levels, k // 32))).repeat(32)
    a = np.empty((k // 512, 16))
    for p in range(k // 512):
        a[p, :8] = np.random.permutation(np.resize(levels, 8))
        for g in range(8):
            far = levels[np.abs(levels - a[p, g]) >= 10]
            a[p, g + 8] = far[np.random.randint(len(far))]
    return np.exp2(a.ravel()).repeat(32)


BF16 = ml_dtypes.bfloat16


def bf(x):
    return np.asarray(x, np.float32).astype(BF16)


def f64(x):
    return np.asarray(x).astype(np.float64)


B, N, D, E = 2, 2048, 4096, 128

EPS = 1e-6
NUM_ITERS = 8
TEMPERATURE = 1.0
FRAC = 0.7
SEP = 2.0


def logsumexp(t, axis):
    m = t.max(axis=axis, keepdims=True)
    return m + np.log(np.exp(t - m).sum(axis=axis, keepdims=True))


def sinkhorn(t):
    t = np.log(np.maximum(t, EPS))
    t = t / TEMPERATURE
    for _ in range(NUM_ITERS):
        t = t - logsumexp(t, -2)
        t = t - logsumexp(t, -1)
    return np.exp(t)


def setup_inputs():
    s = mx_kscale(D)
    p = np.where(np.random.random(D) < 0.5, 1.0, -1.0)
    side = np.where(np.random.random((B, N, 1)) < FRAC, 1.0, -1.0)
    half = np.where(np.arange(E) < E // 2, 1.0, -1.0)[:, None]
    z = np.random.standard_normal((B, N, D))
    z = z - (z @ p)[..., None] * p / D
    g = np.random.standard_normal((E, D))
    g = g - (g @ p)[:, None] * p / D
    return {"x": bf((z + side * p) * s), "w_gate": bf((g / np.sqrt(D) + SEP * half * p / D) / s)}


def reference(x, w_gate):
    gates = mxq(f64(x), 2, "e5m2") @ mxq(f64(w_gate), 1, "e4m3").T
    return sinkhorn(gates)

@@ -1,0 +1,302 @@
+from contextlib import ExitStack
+
+import concourse.mybir as mybir
+from concourse.masks import make_identity
+
+B, N, D, E = 2, 2048, 4096, 128
+EPS = 1e-6
+ROUNDS = 8
+FLOPS = 2 * B * N * D * E
+
+F32 = mybir.dt.float32
+BF16 = mybir.dt.bfloat16
+U32 = mybir.dt.uint32
+U8 = mybir.dt.uint8
+E5M2X4 = mybir.dt.float8_e5m2_x4
+E4M3X4 = mybir.dt.float8_e4m3fn_x4
+ALU = mybir.AluOpType
+ACT = mybir.ActivationFunctionType
+AX = mybir.AxisListType
+
+P = 128
+TILES = N // P
+PAIRS = TILES // 2
+PASS_WORDS = 256
+PASSES = D // 512
+UNIT_PASSES = 4
+UNITS = B * PAIRS * 2
+HALF_STEPS = 2 * ROUNDS - 1
+FIRST_SCALE = 2.0 ** -40
+COLUMN_TARGET = N // E
+LOAD_AHEAD = 4
+SORT_AHEAD = 2
+
+
+def is_sorted_unit(unit):
+    return unit % 4 != 3
+
+
+def tile_sinkhornrouter_kernel(tc, x, w_gate, out):
+    nc = tc.nc
+    with ExitStack() as ctx:
+        keep = ctx.enter_context(tc.tile_pool(name="keep", bufs=1))
+        stream = ctx.enter_context(tc.tile_pool(name="stream", bufs=3))
+        small = ctx.enter_context(tc.tile_pool(name="small", bufs=4))
+        psum = ctx.enter_context(tc.psum_pool(name="psum", bufs=1))
+        ctx.enter_context(nc.allow_low_precision(reason="leading bfloat16 term of a two-term split"))
+        ctx.enter_context(tc.manual_schedule())
+
+        ident32 = keep.tile([P, P], F32, name="ident32")
+        ident16 = keep.tile([P, P], BF16, name="ident16")
+        make_identity(nc, ident32[:])
+        make_identity(nc, ident16[:])
+
+        x_rows = [x[b].rearrange("(p j) k -> p j k", j=TILES) for b in range(B)]
+        out_rows = [out[b].rearrange("(p j) e -> p j e", j=TILES) for b in range(B)]
+
+        k32 = [keep.tile([P, TILES, P], F32, name="k32_%d" % b) for b in range(B)]
+        a_hi = [keep.tile([P, TILES, P], BF16, name="a_hi_%d" % b) for b in range(B)]
+        a_lo = [keep.tile([P, TILES, P], BF16, name="a_lo_%d" % b) for b in range(B)]
+        b_terms = [keep.tile([P, TILES, 2, P], BF16, name="b_terms_%d" % b) for b in range(B)]
+        col_sums = [keep.tile([P, PAIRS], F32, name="col_sums_%d" % b) for b in range(B)]
+        w_codes = keep.tile([P, PASSES * E], U32, name="w_codes", align_bytes=64)
+        w_scales = keep.tile([P, PASSES * E], U8, name="w_scales", align_bytes=64)
+
+        raw, ordered, grouped, x_codes, x_scales, gates = {}, {}, {}, {}, {}, {}
+        col, col_terms, row, row_terms, sums = {}, {}, {}, {}, {}
+
+        def bank_tile(shape, dtype):
+            return psum.tile(shape, dtype, name="bank", tag="bank", bufs=6)
+
+        def transpose_bank(sources, target_words):
+            bank = bank_tile([P, 4, P], F32)
+            for slot, source in enumerate(sources):
+                nc.tensor.transpose(bank[:, slot, :], source, ident32[:])
+            nc.scalar.copy(
+                out=target_words.rearrange("p (t r u) -> p t r u", t=2, u=2),
+                in_=bank[:].rearrange("p (t u) r -> p t r u", u=2),
+            )
+
+        def every_second_word(words, start, u):
+            return words[:, start + u : start + PASS_WORDS : 2]
+
+        def prepare_w():
+            pieces = []
+            for k in range(PASSES // 2):
+                piece = stream.tile([P, 1024], BF16, name="w_piece", tag="w_piece", bufs=PASSES // 2)
+                nc.sync.dma_start(out=piece[:], in_=w_gate[:, 1024 * k : 1024 * (k + 1)])
+                pieces.append(piece)
+            w_grouped = stream.tile([P, 4096], BF16, name="grouped", tag="grouped", bufs=3, align_bytes=64)
+            for k, piece in enumerate(pieces):
+                words = piece[:].bitcast(F32)
+                transpose_bank(
+                    [every_second_word(words, PASS_WORDS * t, u) for t in range(2) for u in range(2)],
+                    w_grouped[:].bitcast(F32)[:, 512 * k : 512 * (k + 1)],
+                )
+            return w_grouped
+
+        def load(unit):
+            pair, half = divmod(unit, 2)
+            b, q = divmod(pair, PAIRS)
+            raw[unit] = stream.tile([P, 2, 2048], BF16, name="raw", tag="raw", bufs=LOAD_AHEAD + 1)
+            nc.sync.dma_start(out=raw[unit][:], in_=x_rows[b][:, 2 * q : 2 * q + 2, 2048 * half : 2048 * (half + 1)])
+
+        def raw_words(unit):
+            return raw[unit][:].rearrange("p t k -> p (t k)").bitcast(F32)
+
+        def sort_words(unit):
+            ordered[unit] = stream.tile([P, 2 * UNIT_PASSES, 2, P], F32, name="ordered", tag="ordered", bufs=SORT_AHEAD + 1)
+            nc.vector.tensor_copy(
+                out=ordered[unit][:],
+                in_=raw_words(unit).rearrange("p (a m u) -> p a u m", m=P, u=2),
+            )
+
+        def transpose_unit(unit):
+            grouped[unit] = stream.tile([P, 4096], BF16, name="grouped", tag="grouped", bufs=3, align_bytes=64)
+            for g in range(UNIT_PASSES):
+                if is_sorted_unit(unit):
+                    sources = [ordered[unit][:, UNIT_PASSES * t + g, u, :] for t in range(2) for u in range(2)]
+                else:
+                    words = raw_words(unit)
+                    sources = [
+                        every_second_word(words, PASS_WORDS * (UNIT_PASSES * t + g), u) for t in range(2) for u in range(2)
+                    ]
+                transpose_bank(sources, grouped[unit][:].bitcast(F32)[:, 512 * g : 512 * (g + 1)])
+
+        def quantize_unit(unit):
+            x_codes[unit] = stream.tile([P, 1024], U32, name="x_codes", tag="x_codes", bufs=4, align_bytes=64)
+            x_scales[unit] = stream.tile([P, 1024], U8, name="x_scales", tag="x_scales", bufs=4, align_bytes=64)
+            nc.vector.quantize_mx(out=x_codes[unit][:].bitcast(E5M2X4), scales=x_scales[unit][:], in_=grouped[unit][:])
+
+        def multiply(pair):
+            gates[pair] = psum.tile([P, 2 * P], F32, name="gates", tag="gates", bufs=1)
+            for g in range(PASSES):
+                unit = 2 * pair + g // UNIT_PASSES
+                tokens = slice(256 * (g % UNIT_PASSES), 256 * (g % UNIT_PASSES + 1))
+                experts = slice(E * g, E * (g + 1))
+                nc.tensor.matmul_mx(
+                    out=gates[pair][:],
+                    lhsT=w_codes[:, experts].bitcast(E4M3X4),
+                    lhsT_scale=w_scales[:, experts],
+                    rhs=x_codes[unit][:, tokens].bitcast(E5M2X4),
+                    rhs_scale=x_scales[unit][:, tokens],
+                    start=(g == 0),
+                    stop=(g == PASSES - 1),
+                )
+
+        def pair_view(tiles, pair):
+            b, q = divmod(pair, PAIRS)
+            return tiles[b][:, 2 * q : 2 * q + 2, :].rearrange("p t n -> p (t n)")
+
+        def clamp(pair):
+            b, q = divmod(pair, PAIRS)
+            nc.vector.tensor_scalar(
+                out=pair_view(k32, pair),
+                in0=gates[pair][:],
+                scalar1=EPS,
+                scalar2=col_sums[b][:, q - 1 : q] if q > 0 else None,
+                op0=ALU.max,
+                op1=ALU.add,
+                accum_out=col_sums[b][:, q : q + 1],
+            )
+
+        def split_hi(pair):
+            nc.vector.tensor_copy(out=pair_view(a_hi, pair), in_=pair_view(k32, pair))
+
+        def split_lo(pair):
+            nc.vector.tensor_tensor(
+                out=pair_view(a_lo, pair), in0=pair_view(k32, pair), in1=pair_view(a_hi, pair), op=ALU.subtract
+            )
+
+        def transpose_terms(pair):
+            b, q = divmod(pair, PAIRS)
+            bank = psum.tile([P, 2, 2, P], BF16, name="terms", tag="terms", bufs=1)
+            for t in range(2):
+                nc.tensor.transpose(bank[:, t, 0, :], a_hi[b][:, 2 * q + t, :], ident16[:])
+                nc.tensor.transpose(bank[:, t, 1, :], a_lo[b][:, 2 * q + t, :], ident16[:])
+            nc.scalar.copy(out=b_terms[b][:, 2 * q : 2 * q + 2, :, :], in_=bank[:])
+
+        def invert(total, width, key):
+            inverse = small.tile([P, width], F32, name="inverse_" + key, tag="inverse_" + key)
+            terms = small.tile([P, width, 2], BF16, name="terms_" + key, tag="terms_" + key)
+            nc.vector.reciprocal(out=inverse[:], in_=total)
+            nc.vector.reciprocal(out=terms[:, :, 0], in_=total)
+            nc.vector.tensor_tensor(out=terms[:, :, 1], in0=inverse[:], in1=terms[:, :, 0], op=ALU.subtract)
+            return inverse, terms
+
+        def first_column_factors(b):
+            total = small.tile([P, 1], F32, name="col_total", tag="col_total")
+            nc.vector.tensor_scalar(
+                out=total[:], in0=col_sums[b][:, PAIRS - 1 : PAIRS], scalar1=FIRST_SCALE, scalar2=None, op0=ALU.mult
+            )
+            col[b], col_terms[b] = invert(total[:], 1, "col")
+
+        def row_step(b):
+            bank = bank_tile([P, TILES, 2], F32)
+            for j in range(TILES):
+                nc.tensor.matmul(bank[:, j, :], lhsT=a_hi[b][:, j, :], rhs=col_terms[b][:, 0, :], start=True, stop=False)
+                nc.tensor.matmul(bank[:, j, :], lhsT=a_lo[b][:, j, :], rhs=col_terms[b][:, 0, :], start=False, stop=True)
+            total = small.tile([P, TILES], F32, name="row_total", tag="row_total")
+            nc.vector.tensor_reduce(out=total[:], in_=bank[:], axis=AX.X, op=ALU.add)
+            row[b], row_terms[b] = invert(total[:], TILES, "row")
+
+        def column_step(b):
+            bank = bank_tile([P, 2], F32)
+            for j in range(TILES):
+                for term in range(2):
+                    nc.tensor.matmul(
+                        bank[:],
+                        lhsT=b_terms[b][:, j, term, :],
+                        rhs=row_terms[b][:, j, :],
+                        start=(j == 0 and term == 0),
+                        stop=(j == TILES - 1 and term == 1),
+                    )
+            total = small.tile([P, 1], F32, name="col_total", tag="col_total")
+            nc.vector.tensor_scalar(
+                out=total[:],
+                in0=bank[:, 0:1],
+                scalar1=bank[:, 1:2],
+                scalar2=1.0 / COLUMN_TARGET,
+                op0=ALU.add,
+                op1=ALU.mult,
+            )
+            col[b], col_terms[b] = invert(total[:], 1, "col")
+
+        def half_step(b, h):
+            if h % 2 == 0:
+                row_step(b)
+            else:
+                column_step(b)
+
+        def finish(b):
+            scaled = stream.tile([P, TILES, P], F32, name="scaled", tag="scaled", bufs=2)
+            result = stream.tile([P, TILES, P], F32, name="result", tag="result", bufs=2)
+            for quarter in range(4):
+                tiles = slice(4 * quarter, 4 * quarter + 4)
+                nc.vector.tensor_scalar(
+                    out=scaled[:, tiles, :], in0=k32[b][:, tiles, :], scalar1=col[b][:], scalar2=None, op0=ALU.mult
+                )
+            for quarter in range(4):
+                tiles = slice(4 * quarter, 4 * quarter + 4)
+                bank = bank_tile([P, 4, P], F32)
+                for t in range(4):
+                    nc.tensor.transpose(bank[:, t, :], scaled[:, 4 * quarter + t, :], ident32[:])
+                if quarter % 2 == 0:
+                    nc.vector.tensor_tensor(
+                        out=result[:, tiles, :],
+                        in0=bank[:],
+                        in1=row[b][:, tiles].unsqueeze(2).to_broadcast([P, 4, P]),
+                        op=ALU.mult,
+                    )
+                else:
+                    for t in range(4):
+                        j = 4 * quarter + t
+                        nc.scalar.activation(out=result[:, j, :], in_=bank[:, t, :], func=ACT.Copy, scale=row[b][:, j : j + 1])
+                nc.sync.dma_start(out=out_rows[b][:, tiles, :], in_=result[:, tiles, :])
+
+        w_grouped = prepare_w()
+        for unit in range(LOAD_AHEAD):
+            load(unit)
+        for unit in range(SORT_AHEAD):
+            if is_sorted_unit(unit):
+                sort_words(unit)
+        nc.vector.quantize_mx(out=w_codes[:].bitcast(E4M3X4), scales=w_scales[:], in_=w_grouped[:])
+
+        def pair_at(step, lag):
+            pair, odd = divmod(step - lag, 2)
+            return pair if odd == 0 and 0 <= pair < B * PAIRS else None
+
+        done0 = 0
+        for step in range(UNITS + 5):
+            if step + LOAD_AHEAD < UNITS:
+                load(step + LOAD_AHEAD)
+            if step + SORT_AHEAD < UNITS and is_sorted_unit(step + SORT_AHEAD):
+                sort_words(step + SORT_AHEAD)
+            if step < UNITS:
+                transpose_unit(step)
+            if pair_at(step, 6) is not None:
+                transpose_terms(pair_at(step, 6))
+            if pair_at(step, 3) is not None:
+                multiply(pair_at(step, 3))
+            if pair_at(step, 5) is not None:
+                split_hi(pair_at(step, 5))
+            if 0 <= step - 1 < UNITS:
+                quantize_unit(step - 1)
+            if pair_at(step, 4) is not None:
+                clamp(pair_at(step, 4))
+            if pair_at(step, 5) is not None:
+                split_lo(pair_at(step, 5))
+            if pair_at(step, 5) in (PAIRS - 1, 2 * PAIRS - 1):
+                first_column_factors(pair_at(step, 5) // PAIRS)
+            if step >= UNITS:
+                half_step(0, done0)
+                done0 += 1
+
+        for h in range(HALF_STEPS):
+            half_step(1, h)
+            if done0 < HALF_STEPS:
+                half_step(0, done0)
+                done0 += 1
+                if done0 == HALF_STEPS:
+                    finish(0)
+        finish(1)

@@ -26,14 +26,12 @@ PASSES = D // 512
 UNIT_PASSES = 4
 UNITS = B * PAIRS * 2
 HALF_STEPS = 2 * ROUNDS - 1
-FIRST_SCALE = 2.0 ** -40
-COLUMN_TARGET = N // E
-LOAD_AHEAD = 4
+FIRST_SCALE = 2.0 ** -60
+SORTED_PASSES = 3
+BURST = 3
+MX_LAG = 10
+LOAD_AHEAD = 5
 SORT_AHEAD = 2
-
-
-def is_sorted_unit(unit):
-    return unit % 4 != 3
 
 
 def tile_sinkhornrouter_kernel(tc, x, w_gate, out):
@@ -63,7 +61,7 @@ def tile_sinkhornrouter_kernel(tc, x, w_gate, out):
         w_scales = keep.tile([P, PASSES * E], U8, name="w_scales", align_bytes=64)
 
         raw, ordered, grouped, x_codes, x_scales, gates = {}, {}, {}, {}, {}, {}
-        col, col_terms, row, row_terms, sums = {}, {}, {}, {}, {}
+        col, col_terms, row, row_terms = {}, {}, {}, {}
 
         def bank_tile(shape, dtype):
             return psum.tile(shape, dtype, name="bank", tag="bank", bufs=6)
@@ -105,44 +103,51 @@ def tile_sinkhornrouter_kernel(tc, x, w_gate, out):
             return raw[unit][:].rearrange("p t k -> p (t k)").bitcast(F32)
 
         def sort_words(unit):
-            ordered[unit] = stream.tile([P, 2 * UNIT_PASSES, 2, P], F32, name="ordered", tag="ordered", bufs=SORT_AHEAD + 1)
+            ordered[unit] = stream.tile([P, 2, SORTED_PASSES, 2, P], F32, name="ordered", tag="ordered", bufs=SORT_AHEAD + 1)
             nc.vector.tensor_copy(
                 out=ordered[unit][:],
-                in_=raw_words(unit).rearrange("p (a m u) -> p a u m", m=P, u=2),
+                in_=raw_words(unit).rearrange("p (t g m u) -> p t g u m", t=2, m=P, u=2)[:, :, 0:SORTED_PASSES, :, :],
             )
 
-        def transpose_unit(unit):
-            grouped[unit] = stream.tile([P, 4096], BF16, name="grouped", tag="grouped", bufs=3, align_bytes=64)
-            for g in range(UNIT_PASSES):
-                if is_sorted_unit(unit):
-                    sources = [ordered[unit][:, UNIT_PASSES * t + g, u, :] for t in range(2) for u in range(2)]
-                else:
-                    words = raw_words(unit)
-                    sources = [
-                        every_second_word(words, PASS_WORDS * (UNIT_PASSES * t + g), u) for t in range(2) for u in range(2)
-                    ]
-                transpose_bank(sources, grouped[unit][:].bitcast(F32)[:, 512 * g : 512 * (g + 1)])
+        def transpose_pass(n):
+            unit, g = divmod(n, UNIT_PASSES)
+            if g == 0:
+                grouped[unit] = stream.tile([P, 4096], BF16, name="grouped", tag="grouped", bufs=3, align_bytes=64)
+            if g < SORTED_PASSES:
+                sources = [ordered[unit][:, t, g, u, :] for t in range(2) for u in range(2)]
+            else:
+                words = raw_words(unit)
+                sources = [every_second_word(words, PASS_WORDS * (UNIT_PASSES * t + g), u) for t in range(2) for u in range(2)]
+            transpose_bank(sources, grouped[unit][:].bitcast(F32)[:, 512 * g : 512 * (g + 1)])
 
-        def quantize_unit(unit):
-            x_codes[unit] = stream.tile([P, 1024], U32, name="x_codes", tag="x_codes", bufs=4, align_bytes=64)
-            x_scales[unit] = stream.tile([P, 1024], U8, name="x_scales", tag="x_scales", bufs=4, align_bytes=64)
-            nc.vector.quantize_mx(out=x_codes[unit][:].bitcast(E5M2X4), scales=x_scales[unit][:], in_=grouped[unit][:])
-
-        def multiply(pair):
-            gates[pair] = psum.tile([P, 2 * P], F32, name="gates", tag="gates", bufs=1)
-            for g in range(PASSES):
-                unit = 2 * pair + g // UNIT_PASSES
-                tokens = slice(256 * (g % UNIT_PASSES), 256 * (g % UNIT_PASSES + 1))
-                experts = slice(E * g, E * (g + 1))
-                nc.tensor.matmul_mx(
-                    out=gates[pair][:],
-                    lhsT=w_codes[:, experts].bitcast(E4M3X4),
-                    lhsT_scale=w_scales[:, experts],
-                    rhs=x_codes[unit][:, tokens].bitcast(E5M2X4),
-                    rhs_scale=x_scales[unit][:, tokens],
-                    start=(g == 0),
-                    stop=(g == PASSES - 1),
+        def quantize_unit(unit, calls):
+            x_codes[unit] = stream.tile([P, 1024], U32, name="x_codes", tag="x_codes", bufs=5, align_bytes=64)
+            x_scales[unit] = stream.tile([P, 1024], U8, name="x_scales", tag="x_scales", bufs=5, align_bytes=64)
+            width = 1024 // calls
+            for call in range(calls):
+                columns = slice(width * call, width * (call + 1))
+                nc.vector.quantize_mx(
+                    out=x_codes[unit][:, columns].bitcast(E5M2X4),
+                    scales=x_scales[unit][:, columns],
+                    in_=grouped[unit][:, 4 * width * call : 4 * width * (call + 1)],
                 )
+
+        def multiply_pass(n):
+            pair, g = divmod(n, PASSES)
+            if g == 0:
+                gates[pair] = psum.tile([P, 2 * P], F32, name="gates", tag="gates", bufs=2)
+            unit = n // UNIT_PASSES
+            tokens = slice(256 * (n % UNIT_PASSES), 256 * (n % UNIT_PASSES + 1))
+            experts = slice(E * g, E * (g + 1))
+            nc.tensor.matmul_mx(
+                out=gates[pair][:],
+                lhsT=w_codes[:, experts].bitcast(E4M3X4),
+                lhsT_scale=w_scales[:, experts],
+                rhs=x_codes[unit][:, tokens].bitcast(E5M2X4),
+                rhs_scale=x_scales[unit][:, tokens],
+                start=(g == 0),
+                stop=(g == PASSES - 1),
+            )
 
         def pair_view(tiles, pair):
             b, q = divmod(pair, PAIRS)
@@ -170,57 +175,51 @@ def tile_sinkhornrouter_kernel(tc, x, w_gate, out):
 
         def transpose_terms(pair):
             b, q = divmod(pair, PAIRS)
-            bank = psum.tile([P, 2, 2, P], BF16, name="terms", tag="terms", bufs=1)
+            bank = bank_tile([P, 2, 2, P], BF16)
             for t in range(2):
                 nc.tensor.transpose(bank[:, t, 0, :], a_hi[b][:, 2 * q + t, :], ident16[:])
                 nc.tensor.transpose(bank[:, t, 1, :], a_lo[b][:, 2 * q + t, :], ident16[:])
             nc.scalar.copy(out=b_terms[b][:, 2 * q : 2 * q + 2, :, :], in_=bank[:])
 
-        def invert(total, width, key):
+        def invert(leading, parts, width, key):
             inverse = small.tile([P, width], F32, name="inverse_" + key, tag="inverse_" + key)
             terms = small.tile([P, width, 2], BF16, name="terms_" + key, tag="terms_" + key)
+            nc.vector.reciprocal(out=terms[:, :, 0], in_=leading)
+            total = leading
+            if parts is not None:
+                summed = small.tile([P, width], F32, name="total_" + key, tag="total_" + key)
+                nc.vector.tensor_reduce(out=summed[:], in_=parts, axis=AX.X, op=ALU.add)
+                total = summed[:]
             nc.vector.reciprocal(out=inverse[:], in_=total)
-            nc.vector.reciprocal(out=terms[:, :, 0], in_=total)
             nc.vector.tensor_tensor(out=terms[:, :, 1], in0=inverse[:], in1=terms[:, :, 0], op=ALU.subtract)
             return inverse, terms
 
         def first_column_factors(b):
-            total = small.tile([P, 1], F32, name="col_total", tag="col_total")
+            total = small.tile([P, 1], F32, name="first_total", tag="first_total")
             nc.vector.tensor_scalar(
                 out=total[:], in0=col_sums[b][:, PAIRS - 1 : PAIRS], scalar1=FIRST_SCALE, scalar2=None, op0=ALU.mult
             )
-            col[b], col_terms[b] = invert(total[:], 1, "col")
+            col[b], col_terms[b] = invert(total[:], None, 1, "col")
 
         def row_step(b):
-            bank = bank_tile([P, TILES, 2], F32)
+            bank = bank_tile([P, TILES, 4], F32)
             for j in range(TILES):
-                nc.tensor.matmul(bank[:, j, :], lhsT=a_hi[b][:, j, :], rhs=col_terms[b][:, 0, :], start=True, stop=False)
-                nc.tensor.matmul(bank[:, j, :], lhsT=a_lo[b][:, j, :], rhs=col_terms[b][:, 0, :], start=False, stop=True)
-            total = small.tile([P, TILES], F32, name="row_total", tag="row_total")
-            nc.vector.tensor_reduce(out=total[:], in_=bank[:], axis=AX.X, op=ALU.add)
-            row[b], row_terms[b] = invert(total[:], TILES, "row")
+                nc.tensor.matmul(bank[:, j, 2:3], lhsT=a_lo[b][:, j, :], rhs=col_terms[b][:, 0, 0:1], start=True, stop=True)
+            for j in range(TILES):
+                nc.tensor.matmul(bank[:, j, 0:2], lhsT=a_hi[b][:, j, :], rhs=col_terms[b][:, 0, :], start=True, stop=True)
+            row[b], row_terms[b] = invert(bank[:, :, 0], bank[:, :, 0:3], TILES, "row")
 
         def column_step(b):
-            bank = bank_tile([P, 2], F32)
+            bank = bank_tile([P, 1, 4], F32)
             for j in range(TILES):
-                for term in range(2):
-                    nc.tensor.matmul(
-                        bank[:],
-                        lhsT=b_terms[b][:, j, term, :],
-                        rhs=row_terms[b][:, j, :],
-                        start=(j == 0 and term == 0),
-                        stop=(j == TILES - 1 and term == 1),
-                    )
-            total = small.tile([P, 1], F32, name="col_total", tag="col_total")
-            nc.vector.tensor_scalar(
-                out=total[:],
-                in0=bank[:, 0:1],
-                scalar1=bank[:, 1:2],
-                scalar2=1.0 / COLUMN_TARGET,
-                op0=ALU.add,
-                op1=ALU.mult,
-            )
-            col[b], col_terms[b] = invert(total[:], 1, "col")
+                nc.tensor.matmul(
+                    bank[:, 0, 2:3], lhsT=b_terms[b][:, j, 1, :], rhs=row_terms[b][:, j, 0:1], start=(j == 0), stop=(j == TILES - 1)
+                )
+            for j in range(TILES):
+                nc.tensor.matmul(
+                    bank[:, 0, 0:2], lhsT=b_terms[b][:, j, 0, :], rhs=row_terms[b][:, j, :], start=(j == 0), stop=(j == TILES - 1)
+                )
+            col[b], col_terms[b] = invert(bank[:, :, 0], bank[:, :, 0:3], 1, "col")
 
         def half_step(b, h):
             if h % 2 == 0:
@@ -258,45 +257,63 @@ def tile_sinkhornrouter_kernel(tc, x, w_gate, out):
         for unit in range(LOAD_AHEAD):
             load(unit)
         for unit in range(SORT_AHEAD):
-            if is_sorted_unit(unit):
-                sort_words(unit)
+            sort_words(unit)
         nc.vector.quantize_mx(out=w_codes[:].bitcast(E4M3X4), scales=w_scales[:], in_=w_grouped[:])
 
-        def pair_at(step, lag):
-            pair, odd = divmod(step - lag, 2)
-            return pair if odd == 0 and 0 <= pair < B * PAIRS else None
+        def pair_at(unit, lag):
+            pair, odd = divmod(unit - lag, 2)
+            return pair if odd == 0 and pair >= 0 else None
 
-        done0 = 0
-        for step in range(UNITS + 5):
-            if step + LOAD_AHEAD < UNITS:
-                load(step + LOAD_AHEAD)
-            if step + SORT_AHEAD < UNITS and is_sorted_unit(step + SORT_AHEAD):
-                sort_words(step + SORT_AHEAD)
-            if step < UNITS:
-                transpose_unit(step)
-            if pair_at(step, 6) is not None:
-                transpose_terms(pair_at(step, 6))
-            if pair_at(step, 3) is not None:
-                multiply(pair_at(step, 3))
-            if pair_at(step, 5) is not None:
-                split_hi(pair_at(step, 5))
-            if 0 <= step - 1 < UNITS:
-                quantize_unit(step - 1)
-            if pair_at(step, 4) is not None:
-                clamp(pair_at(step, 4))
-            if pair_at(step, 5) is not None:
-                split_lo(pair_at(step, 5))
-            if pair_at(step, 5) in (PAIRS - 1, 2 * PAIRS - 1):
-                first_column_factors(pair_at(step, 5) // PAIRS)
-            if step >= UNITS:
-                half_step(0, done0)
-                done0 += 1
+        multiplied = 0
+        for unit in range(UNITS):
+            if unit + LOAD_AHEAD < UNITS:
+                load(unit + LOAD_AHEAD)
+            if unit + SORT_AHEAD < UNITS:
+                sort_words(unit + SORT_AHEAD)
+            if pair_at(unit, 6) is not None:
+                split_hi(pair_at(unit, 6))
+            if unit >= 1:
+                quantize_unit(unit - 1, 1)
+            if pair_at(unit, 5) is not None:
+                clamp(pair_at(unit, 5))
+            if pair_at(unit, 6) is not None:
+                split_lo(pair_at(unit, 6))
+            if pair_at(unit, 7) == PAIRS - 1:
+                first_column_factors(0)
+            for n in range(UNIT_PASSES * unit, UNIT_PASSES * (unit + 1)):
+                transpose_pass(n)
+                if n % UNIT_PASSES == UNIT_PASSES - 1 and pair_at(unit, 7) is not None:
+                    transpose_terms(pair_at(unit, 7))
+                if n % BURST == BURST - 1:
+                    while multiplied <= n - MX_LAG:
+                        multiply_pass(multiplied)
+                        multiplied += 1
+
+        last = B * PAIRS - 1
+        for n in range(multiplied, UNIT_PASSES * (UNITS - 1)):
+            multiply_pass(n)
+        split_hi(last - 2)
+        clamp(last - 1)
+        split_lo(last - 2)
+        split_hi(last - 1)
+        quantize_unit(UNITS - 1, 2)
+        split_lo(last - 1)
+        half_step(0, 0)
+        for n in range(UNIT_PASSES * (UNITS - 1), UNIT_PASSES * UNITS):
+            multiply_pass(n)
+        transpose_terms(last - 2)
+        transpose_terms(last - 1)
+        clamp(last)
+        split_hi(last)
+        first_column_factors(1)
+        split_lo(last)
+        half_step(0, 1)
+        transpose_terms(last)
 
         for h in range(HALF_STEPS):
             half_step(1, h)
-            if done0 < HALF_STEPS:
-                half_step(0, done0)
-                done0 += 1
-                if done0 == HALF_STEPS:
-                    finish(0)
+            if h + 2 < HALF_STEPS:
+                half_step(0, h + 2)
+            if h + 3 == HALF_STEPS:
+                finish(0)
         finish(1)

@@ -27,7 +27,6 @@ UNIT_PASSES = 4
 UNITS = B * PAIRS * 2
 HALF_STEPS = 2 * ROUNDS - 1
 FIRST_SCALE = 2.0 ** -60
-SORTED_PASSES = 3
 BURST = 3
 MX_LAG = 10
 LOAD_AHEAD = 5
@@ -75,20 +74,21 @@ def tile_sinkhornrouter_kernel(tc, x, w_gate, out):
                 in_=bank[:].rearrange("p (t u) r -> p t r u", u=2),
             )
 
-        def every_second_word(words, start, u):
-            return words[:, start + u : start + PASS_WORDS : 2]
-
         def prepare_w():
             pieces = []
             for k in range(PASSES // 2):
                 piece = stream.tile([P, 1024], BF16, name="w_piece", tag="w_piece", bufs=PASSES // 2)
                 nc.sync.dma_start(out=piece[:], in_=w_gate[:, 1024 * k : 1024 * (k + 1)])
                 pieces.append(piece)
-            w_grouped = stream.tile([P, 4096], BF16, name="grouped", tag="grouped", bufs=3, align_bytes=64)
+            w_grouped = stream.tile([P, 4096], BF16, name="grouped", tag="grouped", bufs=4, align_bytes=64)
             for k, piece in enumerate(pieces):
-                words = piece[:].bitcast(F32)
+                w_ordered = stream.tile([P, 2, 2, P], F32, name="w_ordered", tag="w_ordered", bufs=PASSES // 2)
+                nc.vector.tensor_copy(
+                    out=w_ordered[:].rearrange("p u g (b r) -> p u (g b) r", r=8),
+                    in_=piece[:].bitcast(F32).rearrange("p (a u r) -> p u a r", u=2, r=8),
+                )
                 transpose_bank(
-                    [every_second_word(words, PASS_WORDS * t, u) for t in range(2) for u in range(2)],
+                    [w_ordered[:, u, t, :] for t in range(2) for u in range(2)],
                     w_grouped[:].bitcast(F32)[:, 512 * k : 512 * (k + 1)],
                 )
             return w_grouped
@@ -103,21 +103,17 @@ def tile_sinkhornrouter_kernel(tc, x, w_gate, out):
             return raw[unit][:].rearrange("p t k -> p (t k)").bitcast(F32)
 
         def sort_words(unit):
-            ordered[unit] = stream.tile([P, 2, SORTED_PASSES, 2, P], F32, name="ordered", tag="ordered", bufs=SORT_AHEAD + 1)
+            ordered[unit] = stream.tile([P, 2, 2, UNIT_PASSES, P], F32, name="ordered", tag="ordered", bufs=SORT_AHEAD + 1)
             nc.vector.tensor_copy(
-                out=ordered[unit][:],
-                in_=raw_words(unit).rearrange("p (t g m u) -> p t g u m", t=2, m=P, u=2)[:, :, 0:SORTED_PASSES, :, :],
+                out=ordered[unit][:].rearrange("p t u g (b r) -> p t u (g b) r", r=8),
+                in_=raw_words(unit).rearrange("p (t a u r) -> p t u a r", t=2, u=2, r=8),
             )
 
         def transpose_pass(n):
             unit, g = divmod(n, UNIT_PASSES)
             if g == 0:
-                grouped[unit] = stream.tile([P, 4096], BF16, name="grouped", tag="grouped", bufs=3, align_bytes=64)
-            if g < SORTED_PASSES:
-                sources = [ordered[unit][:, t, g, u, :] for t in range(2) for u in range(2)]
-            else:
-                words = raw_words(unit)
-                sources = [every_second_word(words, PASS_WORDS * (UNIT_PASSES * t + g), u) for t in range(2) for u in range(2)]
+                grouped[unit] = stream.tile([P, 4096], BF16, name="grouped", tag="grouped", bufs=4, align_bytes=64)
+            sources = [ordered[unit][:, t, u, g, :] for t in range(2) for u in range(2)]
             transpose_bank(sources, grouped[unit][:].bitcast(F32)[:, 512 * g : 512 * (g + 1)])
 
         def quantize_unit(unit, calls):
@@ -166,7 +162,7 @@ def tile_sinkhornrouter_kernel(tc, x, w_gate, out):
             )
 
         def split_hi(pair):
-            nc.vector.tensor_copy(out=pair_view(a_hi, pair), in_=pair_view(k32, pair))
+            nc.scalar.copy(out=pair_view(a_hi, pair), in_=pair_view(k32, pair))
 
         def split_lo(pair):
             nc.vector.tensor_tensor(
@@ -228,7 +224,7 @@ def tile_sinkhornrouter_kernel(tc, x, w_gate, out):
                 column_step(b)
 
         def finish(b):
-            scaled = stream.tile([P, TILES, P], F32, name="scaled", tag="scaled", bufs=2)
+            scaled = stream.tile([P, TILES, P], F32, name="scaled", tag="scaled", bufs=1)
             result = stream.tile([P, TILES, P], F32, name="result", tag="result", bufs=2)
             for quarter in range(4):
                 tiles = slice(4 * quarter, 4 * quarter + 4)
@@ -240,7 +236,7 @@ def tile_sinkhornrouter_kernel(tc, x, w_gate, out):
                 bank = bank_tile([P, 4, P], F32)
                 for t in range(4):
                     nc.tensor.transpose(bank[:, t, :], scaled[:, 4 * quarter + t, :], ident32[:])
-                if quarter % 2 == 0:
+                if quarter % 2 == 1:
                     nc.vector.tensor_tensor(
                         out=result[:, tiles, :],
                         in0=bank[:],
@@ -270,8 +266,6 @@ def tile_sinkhornrouter_kernel(tc, x, w_gate, out):
                 load(unit + LOAD_AHEAD)
             if unit + SORT_AHEAD < UNITS:
                 sort_words(unit + SORT_AHEAD)
-            if pair_at(unit, 6) is not None:
-                split_hi(pair_at(unit, 6))
             if unit >= 1:
                 quantize_unit(unit - 1, 1)
             if pair_at(unit, 5) is not None:
@@ -288,15 +282,16 @@ def tile_sinkhornrouter_kernel(tc, x, w_gate, out):
                     while multiplied <= n - MX_LAG:
                         multiply_pass(multiplied)
                         multiplied += 1
+            if pair_at(unit, 5) is not None:
+                split_hi(pair_at(unit, 5))
 
         last = B * PAIRS - 1
         for n in range(multiplied, UNIT_PASSES * (UNITS - 1)):
             multiply_pass(n)
-        split_hi(last - 2)
         clamp(last - 1)
-        split_lo(last - 2)
         split_hi(last - 1)
         quantize_unit(UNITS - 1, 2)
+        split_lo(last - 2)
         split_lo(last - 1)
         half_step(0, 0)
         for n in range(UNIT_PASSES * (UNITS - 1), UNIT_PASSES * UNITS):

@@ -27,10 +27,11 @@ UNIT_PASSES = 4
 UNITS = B * PAIRS * 2
 HALF_STEPS = 2 * ROUNDS - 1
 FIRST_SCALE = 2.0 ** -60
-BURST = 3
-MX_LAG = 10
-LOAD_AHEAD = 5
-SORT_AHEAD = 2
+SORTED_PASSES = 3
+BLOCKS = 16
+LOAD_AHEAD = 3
+SORT_AHEAD = 1
+SPLIT_PAIRS = 4
 
 
 def tile_sinkhornrouter_kernel(tc, x, w_gate, out):
@@ -60,7 +61,7 @@ def tile_sinkhornrouter_kernel(tc, x, w_gate, out):
         w_scales = keep.tile([P, PASSES * E], U8, name="w_scales", align_bytes=64)
 
         raw, ordered, grouped, x_codes, x_scales, gates = {}, {}, {}, {}, {}, {}
-        col, col_terms, row, row_terms = {}, {}, {}, {}
+        sums, totals, factors, terms, scaled, results = {}, {}, {}, {}, {}, {}
 
         def bank_tile(shape, dtype):
             return psum.tile(shape, dtype, name="bank", tag="bank", bufs=6)
@@ -74,6 +75,9 @@ def tile_sinkhornrouter_kernel(tc, x, w_gate, out):
                 in_=bank[:].rearrange("p (t u) r -> p t r u", u=2),
             )
 
+        def every_second_word(words, start, u):
+            return words[:, start + u : start + PASS_WORDS : 2]
+
         def prepare_w():
             pieces = []
             for k in range(PASSES // 2):
@@ -82,56 +86,83 @@ def tile_sinkhornrouter_kernel(tc, x, w_gate, out):
                 pieces.append(piece)
             w_grouped = stream.tile([P, 4096], BF16, name="grouped", tag="grouped", bufs=4, align_bytes=64)
             for k, piece in enumerate(pieces):
-                w_ordered = stream.tile([P, 2, 2, P], F32, name="w_ordered", tag="w_ordered", bufs=PASSES // 2)
+                words = piece[:].bitcast(F32)
+                count = len([g for g in (2 * k, 2 * k + 1) if g % UNIT_PASSES < SORTED_PASSES])
+                w_ordered = stream.tile([P, 2, count, P], F32, name="w_ordered", tag="w_ordered", bufs=PASSES // 2)
                 nc.vector.tensor_copy(
                     out=w_ordered[:].rearrange("p u g (b r) -> p u (g b) r", r=8),
-                    in_=piece[:].bitcast(F32).rearrange("p (a u r) -> p u a r", u=2, r=8),
+                    in_=words.rearrange("p (a u r) -> p u a r", u=2, r=8)[:, :, 0 : BLOCKS * count, :],
                 )
-                transpose_bank(
-                    [w_ordered[:, u, t, :] for t in range(2) for u in range(2)],
-                    w_grouped[:].bitcast(F32)[:, 512 * k : 512 * (k + 1)],
-                )
+                sources = [
+                    w_ordered[:, u, t, :] if t < count else every_second_word(words, PASS_WORDS * t, u)
+                    for t in range(2)
+                    for u in range(2)
+                ]
+                transpose_bank(sources, w_grouped[:].bitcast(F32)[:, 512 * k : 512 * (k + 1)])
             return w_grouped
 
-        def load(unit):
-            pair, half = divmod(unit, 2)
-            b, q = divmod(pair, PAIRS)
-            raw[unit] = stream.tile([P, 2, 2048], BF16, name="raw", tag="raw", bufs=LOAD_AHEAD + 1)
-            nc.sync.dma_start(out=raw[unit][:], in_=x_rows[b][:, 2 * q : 2 * q + 2, 2048 * half : 2048 * (half + 1)])
+        def wide_tile(shape, dtype):
+            return stream.tile(shape, dtype, name="wide", tag="wide", bufs=LOAD_AHEAD + 1)
 
-        def raw_words(unit):
-            return raw[unit][:].rearrange("p t k -> p (t k)").bitcast(F32)
+        def loaded_by_halves(pair):
+            return pair < SPLIT_PAIRS or pair == B * PAIRS - 1
+
+        def load(pair):
+            b, q = divmod(pair, PAIRS)
+            raw[pair] = wide_tile([P, 2, D], BF16)
+            for part in range(2):
+                if loaded_by_halves(pair):
+                    nc.sync.dma_start(
+                        out=raw[pair][:, part, :].rearrange("p (t k) -> p t k", t=2),
+                        in_=x_rows[b][:, 2 * q : 2 * q + 2, D // 2 * part : D // 2 * (part + 1)],
+                    )
+                else:
+                    nc.sync.dma_start(out=raw[pair][:, part, :], in_=x_rows[b][:, 2 * q + part, :])
+
+        def unit_words(unit):
+            pair, half = divmod(unit, 2)
+            words = raw[pair][:].rearrange("p a k -> p (a k)").bitcast(F32)
+            layout = "p (h t w) -> p h t w" if loaded_by_halves(pair) else "p (t h w) -> p h t w"
+            return words.rearrange(layout, h=2, t=2)[:, half, :, :]
 
         def sort_words(unit):
-            ordered[unit] = stream.tile([P, 2, 2, UNIT_PASSES, P], F32, name="ordered", tag="ordered", bufs=SORT_AHEAD + 1)
+            ordered[unit] = stream.tile([P, 2, 2, SORTED_PASSES, P], F32, name="ordered", tag="ordered", bufs=3)
             nc.vector.tensor_copy(
                 out=ordered[unit][:].rearrange("p t u g (b r) -> p t u (g b) r", r=8),
-                in_=raw_words(unit).rearrange("p (t a u r) -> p t u a r", t=2, u=2, r=8),
+                in_=unit_words(unit).rearrange("p t (a u r) -> p t u a r", u=2, r=8)[:, :, :, 0 : BLOCKS * SORTED_PASSES, :],
             )
 
-        def transpose_pass(n):
-            unit, g = divmod(n, UNIT_PASSES)
-            if g == 0:
-                grouped[unit] = stream.tile([P, 4096], BF16, name="grouped", tag="grouped", bufs=4, align_bytes=64)
-            sources = [ordered[unit][:, t, u, g, :] for t in range(2) for u in range(2)]
-            transpose_bank(sources, grouped[unit][:].bitcast(F32)[:, 512 * g : 512 * (g + 1)])
+        def transpose_unit(unit):
+            grouped[unit] = stream.tile([P, 4096], BF16, name="grouped", tag="grouped", bufs=4, align_bytes=64)
+            for g in range(UNIT_PASSES):
+                sources = [
+                    ordered[unit][:, t, u, g, :]
+                    if g < SORTED_PASSES
+                    else every_second_word(unit_words(unit)[:, t, :], PASS_WORDS * g, u)
+                    for t in range(2)
+                    for u in range(2)
+                ]
+                transpose_bank(sources, grouped[unit][:].bitcast(F32)[:, 512 * g : 512 * (g + 1)])
 
-        def quantize_unit(unit, calls):
-            x_codes[unit] = stream.tile([P, 1024], U32, name="x_codes", tag="x_codes", bufs=5, align_bytes=64)
-            x_scales[unit] = stream.tile([P, 1024], U8, name="x_scales", tag="x_scales", bufs=5, align_bytes=64)
-            width = 1024 // calls
-            for call in range(calls):
-                columns = slice(width * call, width * (call + 1))
-                nc.vector.quantize_mx(
-                    out=x_codes[unit][:, columns].bitcast(E5M2X4),
-                    scales=x_scales[unit][:, columns],
-                    in_=grouped[unit][:, 4 * width * call : 4 * width * (call + 1)],
-                )
+        def quantize(unit, first_pass, passes):
+            if first_pass == 0:
+                x_codes[unit] = stream.tile([P, 1024], U32, name="x_codes", tag="x_codes", bufs=4, align_bytes=64)
+                x_scales[unit] = stream.tile([P, 1024], U8, name="x_scales", tag="x_scales", bufs=4, align_bytes=64)
+            columns = slice(256 * first_pass, 256 * (first_pass + passes))
+            nc.vector.quantize_mx(
+                out=x_codes[unit][:, columns].bitcast(E5M2X4),
+                scales=x_scales[unit][:, columns],
+                in_=grouped[unit][:, 4 * columns.start : 4 * columns.stop],
+            )
+
+        def multiply_unit(unit):
+            for n in range(UNIT_PASSES * unit, UNIT_PASSES * (unit + 1)):
+                multiply_pass(n)
 
         def multiply_pass(n):
             pair, g = divmod(n, PASSES)
             if g == 0:
-                gates[pair] = psum.tile([P, 2 * P], F32, name="gates", tag="gates", bufs=2)
+                gates[pair] = psum.tile([P, 2 * P], F32, name="gates", tag="gates", bufs=1)
             unit = n // UNIT_PASSES
             tokens = slice(256 * (n % UNIT_PASSES), 256 * (n % UNIT_PASSES + 1))
             experts = slice(E * g, E * (g + 1))
@@ -162,7 +193,7 @@ def tile_sinkhornrouter_kernel(tc, x, w_gate, out):
             )
 
         def split_hi(pair):
-            nc.scalar.copy(out=pair_view(a_hi, pair), in_=pair_view(k32, pair))
+            nc.vector.tensor_copy(out=pair_view(a_hi, pair), in_=pair_view(k32, pair))
 
         def split_lo(pair):
             nc.vector.tensor_tensor(
@@ -177,81 +208,94 @@ def tile_sinkhornrouter_kernel(tc, x, w_gate, out):
                 nc.tensor.transpose(bank[:, t, 1, :], a_lo[b][:, 2 * q + t, :], ident16[:])
             nc.scalar.copy(out=b_terms[b][:, 2 * q : 2 * q + 2, :, :], in_=bank[:])
 
-        def invert(leading, parts, width, key):
-            inverse = small.tile([P, width], F32, name="inverse_" + key, tag="inverse_" + key)
-            terms = small.tile([P, width, 2], BF16, name="terms_" + key, tag="terms_" + key)
-            nc.vector.reciprocal(out=terms[:, :, 0], in_=leading)
-            total = leading
-            if parts is not None:
-                summed = small.tile([P, width], F32, name="total_" + key, tag="total_" + key)
-                nc.vector.tensor_reduce(out=summed[:], in_=parts, axis=AX.X, op=ALU.add)
-                total = summed[:]
-            nc.vector.reciprocal(out=inverse[:], in_=total)
-            nc.vector.tensor_tensor(out=terms[:, :, 1], in0=inverse[:], in1=terms[:, :, 0], op=ALU.subtract)
-            return inverse, terms
-
-        def first_column_factors(b):
-            total = small.tile([P, 1], F32, name="first_total", tag="first_total")
-            nc.vector.tensor_scalar(
-                out=total[:], in0=col_sums[b][:, PAIRS - 1 : PAIRS], scalar1=FIRST_SCALE, scalar2=None, op0=ALU.mult
-            )
-            col[b], col_terms[b] = invert(total[:], None, 1, "col")
-
-        def row_step(b):
-            bank = bank_tile([P, TILES, 4], F32)
-            for j in range(TILES):
-                nc.tensor.matmul(bank[:, j, 2:3], lhsT=a_lo[b][:, j, :], rhs=col_terms[b][:, 0, 0:1], start=True, stop=True)
-            for j in range(TILES):
-                nc.tensor.matmul(bank[:, j, 0:2], lhsT=a_hi[b][:, j, :], rhs=col_terms[b][:, 0, :], start=True, stop=True)
-            row[b], row_terms[b] = invert(bank[:, :, 0], bank[:, :, 0:3], TILES, "row")
-
-        def column_step(b):
-            bank = bank_tile([P, 1, 4], F32)
-            for j in range(TILES):
-                nc.tensor.matmul(
-                    bank[:, 0, 2:3], lhsT=b_terms[b][:, j, 1, :], rhs=row_terms[b][:, j, 0:1], start=(j == 0), stop=(j == TILES - 1)
-                )
-            for j in range(TILES):
-                nc.tensor.matmul(
-                    bank[:, 0, 0:2], lhsT=b_terms[b][:, j, 0, :], rhs=row_terms[b][:, j, :], start=(j == 0), stop=(j == TILES - 1)
-                )
-            col[b], col_terms[b] = invert(bank[:, :, 0], bank[:, :, 0:3], 1, "col")
-
-        def half_step(b, h):
-            if h % 2 == 0:
-                row_step(b)
-            else:
-                column_step(b)
-
-        def finish(b):
-            scaled = stream.tile([P, TILES, P], F32, name="scaled", tag="scaled", bufs=1)
-            result = stream.tile([P, TILES, P], F32, name="result", tag="result", bufs=2)
-            for quarter in range(4):
-                tiles = slice(4 * quarter, 4 * quarter + 4)
+        def invert_leading(b, h):
+            width = TILES if h % 2 == 0 else 1
+            factors[b, h] = small.tile([P, width], F32, name="factors", tag="factors", bufs=8)
+            terms[b, h] = small.tile([P, 2, TILES], BF16, name="terms", tag="terms", bufs=8)
+            totals[b, h] = small.tile([P, width], F32, name="totals", tag="totals", bufs=8)
+            if h < 0:
                 nc.vector.tensor_scalar(
-                    out=scaled[:, tiles, :], in0=k32[b][:, tiles, :], scalar1=col[b][:], scalar2=None, op0=ALU.mult
+                    out=totals[b, h][:], in0=col_sums[b][:, PAIRS - 1 : PAIRS], scalar1=FIRST_SCALE, scalar2=None, op0=ALU.mult
                 )
-            for quarter in range(4):
-                tiles = slice(4 * quarter, 4 * quarter + 4)
-                bank = bank_tile([P, 4, P], F32)
-                for t in range(4):
-                    nc.tensor.transpose(bank[:, t, :], scaled[:, 4 * quarter + t, :], ident32[:])
-                if quarter % 2 == 1:
-                    nc.vector.tensor_tensor(
-                        out=result[:, tiles, :],
-                        in0=bank[:],
-                        in1=row[b][:, tiles].unsqueeze(2).to_broadcast([P, 4, P]),
-                        op=ALU.mult,
+                nc.vector.reciprocal(out=terms[b, h][:, 0, 0:width], in_=totals[b, h][:])
+            else:
+                nc.vector.reciprocal(out=terms[b, h][:, 0, 0:width], in_=sums[b, h][:, :, 0])
+                nc.vector.tensor_reduce(out=totals[b, h][:], in_=sums[b, h][:, :, 0:3], axis=AX.X, op=ALU.add)
+
+        def invert_total(b, h):
+            nc.vector.reciprocal(out=factors[b, h][:], in_=totals[b, h][:])
+
+        def invert_remainder(b, h):
+            width = TILES if h % 2 == 0 else 1
+            nc.vector.tensor_tensor(
+                out=terms[b, h][:, 1, 0:width], in0=factors[b, h][:], in1=terms[b, h][:, 0, 0:width], op=ALU.subtract
+            )
+
+        def invert(b, h):
+            invert_leading(b, h)
+            invert_total(b, h)
+            invert_remainder(b, h)
+
+        def sum_part(b, h, part):
+            is_row_step = h % 2 == 0
+            if part == 0:
+                shape = [P, TILES if is_row_step else 1, 4]
+                sums[b, h] = psum.tile(shape, F32, name="sums", tag="sums", bufs=1) if b == 0 else bank_tile(shape, F32)
+            out_columns = slice(2, 3) if part == 0 else slice(0, 2)
+            used_terms = slice(0, 1) if part == 0 else slice(0, 2)
+            for j in range(TILES):
+                if is_row_step:
+                    nc.tensor.matmul(
+                        sums[b, h][:, j, out_columns],
+                        lhsT=(a_lo if part == 0 else a_hi)[b][:, j, :],
+                        rhs=terms[b, h - 1][:, used_terms, 0],
+                        start=True,
+                        stop=True,
                     )
                 else:
-                    for t in range(4):
-                        j = 4 * quarter + t
-                        nc.scalar.activation(out=result[:, j, :], in_=bank[:, t, :], func=ACT.Copy, scale=row[b][:, j : j + 1])
-                nc.sync.dma_start(out=out_rows[b][:, tiles, :], in_=result[:, tiles, :])
+                    nc.tensor.matmul(
+                        sums[b, h][:, 0, out_columns],
+                        lhsT=b_terms[b][:, j, 1 - part, :],
+                        rhs=terms[b, h - 1][:, used_terms, j],
+                        start=(j == 0),
+                        stop=(j == TILES - 1),
+                    )
+
+        def scale_columns(b, quarters_on_vector):
+            column = factors[b, HALF_STEPS - 2][:]
+            scaled[b] = wide_tile([P, TILES, P], F32)
+            results[b] = wide_tile([P, TILES, P], F32)
+            for quarter in range(4):
+                tiles = slice(4 * quarter, 4 * quarter + 4)
+                if quarter < quarters_on_vector:
+                    nc.vector.tensor_scalar(
+                        out=scaled[b][:, tiles, :], in0=k32[b][:, tiles, :], scalar1=column, scalar2=None, op0=ALU.mult
+                    )
+                else:
+                    nc.scalar.activation(out=scaled[b][:, tiles, :], in_=k32[b][:, tiles, :], func=ACT.Copy, scale=column)
+
+        def finish_quarter(b, quarter, on_vector):
+            row = factors[b, HALF_STEPS - 1]
+            tiles = slice(4 * quarter, 4 * quarter + 4)
+            bank = bank_tile([P, 4, P], F32)
+            for t in range(4):
+                nc.tensor.transpose(bank[:, t, :], scaled[b][:, 4 * quarter + t, :], ident32[:])
+            if on_vector:
+                nc.vector.tensor_tensor(
+                    out=results[b][:, tiles, :],
+                    in0=bank[:],
+                    in1=row[:, tiles].unsqueeze(2).to_broadcast([P, 4, P]),
+                    op=ALU.mult,
+                )
+            else:
+                for t in range(4):
+                    j = 4 * quarter + t
+                    nc.scalar.activation(out=results[b][:, j, :], in_=bank[:, t, :], func=ACT.Copy, scale=row[:, j : j + 1])
+            nc.sync.dma_start(out=out_rows[b][:, tiles, :], in_=results[b][:, tiles, :])
 
         w_grouped = prepare_w()
-        for unit in range(LOAD_AHEAD):
-            load(unit)
+        for pair in range(LOAD_AHEAD):
+            load(pair)
         for unit in range(SORT_AHEAD):
             sort_words(unit)
         nc.vector.quantize_mx(out=w_codes[:].bitcast(E4M3X4), scales=w_scales[:], in_=w_grouped[:])
@@ -260,55 +304,83 @@ def tile_sinkhornrouter_kernel(tc, x, w_gate, out):
             pair, odd = divmod(unit - lag, 2)
             return pair if odd == 0 and pair >= 0 else None
 
-        multiplied = 0
+        first_woven_unit = 2 * (PAIRS - 1) + 6
         for unit in range(UNITS):
-            if unit + LOAD_AHEAD < UNITS:
-                load(unit + LOAD_AHEAD)
+            woven = unit - first_woven_unit
+            inverting = woven // 2 - 1 if woven >= 0 and woven % 2 == 0 else None
+            if unit % 2 == 0 and unit // 2 + LOAD_AHEAD < B * PAIRS:
+                load(unit // 2 + LOAD_AHEAD)
             if unit + SORT_AHEAD < UNITS:
                 sort_words(unit + SORT_AHEAD)
-            if unit >= 1:
-                quantize_unit(unit - 1, 1)
-            if pair_at(unit, 5) is not None:
-                clamp(pair_at(unit, 5))
-            if pair_at(unit, 6) is not None:
-                split_lo(pair_at(unit, 6))
-            if pair_at(unit, 7) == PAIRS - 1:
-                first_column_factors(0)
-            for n in range(UNIT_PASSES * unit, UNIT_PASSES * (unit + 1)):
-                transpose_pass(n)
-                if n % UNIT_PASSES == UNIT_PASSES - 1 and pair_at(unit, 7) is not None:
-                    transpose_terms(pair_at(unit, 7))
-                if n % BURST == BURST - 1:
-                    while multiplied <= n - MX_LAG:
-                        multiply_pass(multiplied)
-                        multiplied += 1
             if pair_at(unit, 5) is not None:
                 split_hi(pair_at(unit, 5))
+            if inverting is not None:
+                invert_leading(0, inverting)
+            if unit >= 1:
+                quantize(unit - 1, 0, UNIT_PASSES)
+            if inverting is not None:
+                invert_total(0, inverting)
+            if pair_at(unit, 4) is not None:
+                clamp(pair_at(unit, 4))
+            if pair_at(unit, 5) is not None:
+                split_lo(pair_at(unit, 5))
+            if inverting is not None:
+                invert_remainder(0, inverting)
+            transpose_unit(unit)
+            if pair_at(unit, 6) is not None:
+                transpose_terms(pair_at(unit, 6))
+            if woven >= 0:
+                sum_part(0, woven // 2, woven % 2)
+            if pair_at(unit, 3) is not None:
+                multiply_unit(unit - 3)
+                multiply_unit(unit - 2)
 
         last = B * PAIRS - 1
-        for n in range(multiplied, UNIT_PASSES * (UNITS - 1)):
-            multiply_pass(n)
+        step0 = (UNITS - first_woven_unit) // 2
+        invert(0, step0 - 1)
         clamp(last - 1)
-        split_hi(last - 1)
-        quantize_unit(UNITS - 1, 2)
-        split_lo(last - 2)
-        split_lo(last - 1)
-        half_step(0, 0)
-        for n in range(UNIT_PASSES * (UNITS - 1), UNIT_PASSES * UNITS):
-            multiply_pass(n)
         transpose_terms(last - 2)
+        multiply_unit(UNITS - 2)
+        sum_part(0, step0, 0)
+        sum_part(0, step0, 1)
+        quantize(UNITS - 1, 0, 2)
+        split_hi(last - 1)
+        quantize(UNITS - 1, 2, 2)
+        multiply_unit(UNITS - 1)
+        invert_leading(0, step0)
+        split_lo(last - 1)
+        invert_total(0, step0)
+        invert_remainder(0, step0)
         transpose_terms(last - 1)
+        sum_part(0, step0 + 1, 0)
+        sum_part(0, step0 + 1, 1)
         clamp(last)
         split_hi(last)
-        first_column_factors(1)
+        invert_leading(1, -1)
         split_lo(last)
-        half_step(0, 1)
-        transpose_terms(last)
+        invert_total(1, -1)
+        invert_remainder(1, -1)
+        invert(0, step0 + 1)
 
+        parts_left = [(h, part) for h in range(step0 + 2, HALF_STEPS) for part in range(2)]
+        part_gaps = HALF_STEPS - 1 - 4
+        double_gaps = len(parts_left) - part_gaps
         for h in range(HALF_STEPS):
-            half_step(1, h)
-            if h + 2 < HALF_STEPS:
-                half_step(0, h + 2)
-            if h + 3 == HALF_STEPS:
-                finish(0)
-        finish(1)
+            sum_part(1, h, 0)
+            sum_part(1, h, 1)
+            if h == 0:
+                transpose_terms(last)
+            invert(1, h)
+            if h == HALF_STEPS - 2:
+                scale_columns(1, 2)
+            if h < part_gaps:
+                for h0, part in parts_left[h + min(h, double_gaps) : h + 1 + min(h + 1, double_gaps)]:
+                    sum_part(0, h0, part)
+                    if part == 1:
+                        invert(0, h0)
+                        if h0 == HALF_STEPS - 2:
+                            scale_columns(0, 0)
+            elif h < HALF_STEPS - 1:
+                finish_quarter(0, h - part_gaps, False)
+        for quarter in range(4):
+            finish_quarter(1, quarter, quarter % 2 == 1)

@@ -27,7 +27,7 @@ UNIT_PASSES = 4
 UNITS = B * PAIRS * 2
 HALF_STEPS = 2 * ROUNDS - 1
 FIRST_SCALE = 2.0 ** -60
-SORTED_PASSES = 3
+SORTED_PASSES = 7
 BLOCKS = 16
 LOAD_AHEAD = 3
 SORT_AHEAD = 1
@@ -64,7 +64,7 @@ def tile_sinkhornrouter_kernel(tc, x, w_gate, out):
         sums, totals, factors, terms, scaled, results = {}, {}, {}, {}, {}, {}
 
         def bank_tile(shape, dtype):
-            return psum.tile(shape, dtype, name="bank", tag="bank", bufs=6)
+            return psum.tile(shape, dtype, name="bank", tag="bank", bufs=5)
 
         def transpose_bank(sources, target_words):
             bank = bank_tile([P, 4, P], F32)
@@ -87,7 +87,7 @@ def tile_sinkhornrouter_kernel(tc, x, w_gate, out):
             w_grouped = stream.tile([P, 4096], BF16, name="grouped", tag="grouped", bufs=4, align_bytes=64)
             for k, piece in enumerate(pieces):
                 words = piece[:].bitcast(F32)
-                count = len([g for g in (2 * k, 2 * k + 1) if g % UNIT_PASSES < SORTED_PASSES])
+                count = len([g for g in (2 * k, 2 * k + 1) if g < SORTED_PASSES])
                 w_ordered = stream.tile([P, 2, count, P], F32, name="w_ordered", tag="w_ordered", bufs=PASSES // 2)
                 nc.vector.tensor_copy(
                     out=w_ordered[:].rearrange("p u g (b r) -> p u (g b) r", r=8),
@@ -125,11 +125,14 @@ def tile_sinkhornrouter_kernel(tc, x, w_gate, out):
             layout = "p (h t w) -> p h t w" if loaded_by_halves(pair) else "p (t h w) -> p h t w"
             return words.rearrange(layout, h=2, t=2)[:, half, :, :]
 
+        def sorted_in(unit):
+            return min(UNIT_PASSES, SORTED_PASSES - UNIT_PASSES * (unit % 2))
+
         def sort_words(unit):
-            ordered[unit] = stream.tile([P, 2, 2, SORTED_PASSES, P], F32, name="ordered", tag="ordered", bufs=3)
+            ordered[unit] = stream.tile([P, 2, 2, sorted_in(unit), P], F32, name="ordered", tag="ordered", bufs=3)
             nc.vector.tensor_copy(
                 out=ordered[unit][:].rearrange("p t u g (b r) -> p t u (g b) r", r=8),
-                in_=unit_words(unit).rearrange("p t (a u r) -> p t u a r", u=2, r=8)[:, :, :, 0 : BLOCKS * SORTED_PASSES, :],
+                in_=unit_words(unit).rearrange("p t (a u r) -> p t u a r", u=2, r=8)[:, :, :, 0 : BLOCKS * sorted_in(unit), :],
             )
 
         def transpose_unit(unit):
@@ -137,7 +140,7 @@ def tile_sinkhornrouter_kernel(tc, x, w_gate, out):
             for g in range(UNIT_PASSES):
                 sources = [
                     ordered[unit][:, t, u, g, :]
-                    if g < SORTED_PASSES
+                    if g < sorted_in(unit)
                     else every_second_word(unit_words(unit)[:, t, :], PASS_WORDS * g, u)
                     for t in range(2)
                     for u in range(2)
@@ -162,7 +165,7 @@ def tile_sinkhornrouter_kernel(tc, x, w_gate, out):
         def multiply_pass(n):
             pair, g = divmod(n, PASSES)
             if g == 0:
-                gates[pair] = psum.tile([P, 2 * P], F32, name="gates", tag="gates", bufs=1)
+                gates[pair] = psum.tile([P, 2 * P], F32, name="gates", tag="gates", bufs=2)
             unit = n // UNIT_PASSES
             tokens = slice(256 * (n % UNIT_PASSES), 256 * (n % UNIT_PASSES + 1))
             experts = slice(E * g, E * (g + 1))
@@ -193,7 +196,7 @@ def tile_sinkhornrouter_kernel(tc, x, w_gate, out):
             )
 
         def split_hi(pair):
-            nc.vector.tensor_copy(out=pair_view(a_hi, pair), in_=pair_view(k32, pair))
+            nc.scalar.copy(out=pair_view(a_hi, pair), in_=pair_view(k32, pair))
 
         def split_lo(pair):
             nc.vector.tensor_tensor(
@@ -312,8 +315,6 @@ def tile_sinkhornrouter_kernel(tc, x, w_gate, out):
                 load(unit // 2 + LOAD_AHEAD)
             if unit + SORT_AHEAD < UNITS:
                 sort_words(unit + SORT_AHEAD)
-            if pair_at(unit, 5) is not None:
-                split_hi(pair_at(unit, 5))
             if inverting is not None:
                 invert_leading(0, inverting)
             if unit >= 1:
@@ -331,9 +332,10 @@ def tile_sinkhornrouter_kernel(tc, x, w_gate, out):
                 transpose_terms(pair_at(unit, 6))
             if woven >= 0:
                 sum_part(0, woven // 2, woven % 2)
-            if pair_at(unit, 3) is not None:
-                multiply_unit(unit - 3)
+            if unit >= 2:
                 multiply_unit(unit - 2)
+            if pair_at(unit, 4) is not None:
+                split_hi(pair_at(unit, 4))
 
         last = B * PAIRS - 1
         step0 = (UNITS - first_woven_unit) // 2

from contextlib import ExitStack

import concourse.mybir as mybir
from concourse.masks import make_identity

B, N, D, E = 2, 2048, 4096, 128
EPS = 1e-6
ROUNDS = 8
FLOPS = 2 * B * N * D * E

F32 = mybir.dt.float32
BF16 = mybir.dt.bfloat16
U32 = mybir.dt.uint32
U8 = mybir.dt.uint8
E5M2X4 = mybir.dt.float8_e5m2_x4
E4M3X4 = mybir.dt.float8_e4m3fn_x4
ALU = mybir.AluOpType
ACT = mybir.ActivationFunctionType
AX = mybir.AxisListType

P = 128
TILES = N // P
PAIRS = TILES // 2
PASS_WORDS = 256
PASSES = D // 512
UNIT_PASSES = 4
UNITS = B * PAIRS * 2
HALF_STEPS = 2 * ROUNDS - 1
FIRST_SCALE = 2.0 ** -60
SORTED_PASSES = 7
BLOCKS = 16
LOAD_AHEAD = 3
SORT_AHEAD = 1
SPLIT_PAIRS = 4


def tile_sinkhornrouter_kernel(tc, x, w_gate, out):
    nc = tc.nc
    with ExitStack() as ctx:
        keep = ctx.enter_context(tc.tile_pool(name="keep", bufs=1))
        stream = ctx.enter_context(tc.tile_pool(name="stream", bufs=3))
        small = ctx.enter_context(tc.tile_pool(name="small", bufs=4))
        psum = ctx.enter_context(tc.psum_pool(name="psum", bufs=1))
        ctx.enter_context(nc.allow_low_precision(reason="leading bfloat16 term of a two-term split"))
        ctx.enter_context(tc.manual_schedule())

        ident32 = keep.tile([P, P], F32, name="ident32")
        ident16 = keep.tile([P, P], BF16, name="ident16")
        make_identity(nc, ident32[:])
        make_identity(nc, ident16[:])

        x_rows = [x[b].rearrange("(p j) k -> p j k", j=TILES) for b in range(B)]
        out_rows = [out[b].rearrange("(p j) e -> p j e", j=TILES) for b in range(B)]

        k32 = [keep.tile([P, TILES, P], F32, name="k32_%d" % b) for b in range(B)]
        a_hi = [keep.tile([P, TILES, P], BF16, name="a_hi_%d" % b) for b in range(B)]
        a_lo = [keep.tile([P, TILES, P], BF16, name="a_lo_%d" % b) for b in range(B)]
        b_terms = [keep.tile([P, TILES, 2, P], BF16, name="b_terms_%d" % b) for b in range(B)]
        col_sums = [keep.tile([P, PAIRS], F32, name="col_sums_%d" % b) for b in range(B)]
        w_codes = keep.tile([P, PASSES * E], U32, name="w_codes", align_bytes=64)
        w_scales = keep.tile([P, PASSES * E], U8, name="w_scales", align_bytes=64)

        raw, ordered, grouped, x_codes, x_scales, gates = {}, {}, {}, {}, {}, {}
        sums, totals, factors, terms, scaled, results = {}, {}, {}, {}, {}, {}

        def bank_tile(shape, dtype):
            return psum.tile(shape, dtype, name="bank", tag="bank", bufs=5)

        def transpose_bank(sources, target_words):
            bank = bank_tile([P, 4, P], F32)
            for slot, source in enumerate(sources):
                nc.tensor.transpose(bank[:, slot, :], source, ident32[:])
            nc.scalar.copy(
                out=target_words.rearrange("p (t r u) -> p t r u", t=2, u=2),
                in_=bank[:].rearrange("p (t u) r -> p t r u", u=2),
            )

        def every_second_word(words, start, u):
            return words[:, start + u : start + PASS_WORDS : 2]

        def prepare_w():
            pieces = []
            for k in range(PASSES // 2):
                piece = stream.tile([P, 1024], BF16, name="w_piece", tag="w_piece", bufs=PASSES // 2)
                nc.sync.dma_start(out=piece[:], in_=w_gate[:, 1024 * k : 1024 * (k + 1)])
                pieces.append(piece)
            w_grouped = stream.tile([P, 4096], BF16, name="grouped", tag="grouped", bufs=4, align_bytes=64)
            for k, piece in enumerate(pieces):
                words = piece[:].bitcast(F32)
                count = len([g for g in (2 * k, 2 * k + 1) if g < SORTED_PASSES])
                w_ordered = stream.tile([P, 2, count, P], F32, name="w_ordered", tag="w_ordered", bufs=PASSES // 2)
                nc.vector.tensor_copy(
                    out=w_ordered[:].rearrange("p u g (b r) -> p u (g b) r", r=8),
                    in_=words.rearrange("p (a u r) -> p u a r", u=2, r=8)[:, :, 0 : BLOCKS * count, :],
                )
                sources = [
                    w_ordered[:, u, t, :] if t < count else every_second_word(words, PASS_WORDS * t, u)
                    for t in range(2)
                    for u in range(2)
                ]
                transpose_bank(sources, w_grouped[:].bitcast(F32)[:, 512 * k : 512 * (k + 1)])
            return w_grouped

        def wide_tile(shape, dtype):
            return stream.tile(shape, dtype, name="wide", tag="wide", bufs=LOAD_AHEAD + 1)

        def loaded_by_halves(pair):
            return pair < SPLIT_PAIRS or pair == B * PAIRS - 1

        def load(pair):
            b, q = divmod(pair, PAIRS)
            raw[pair] = wide_tile([P, 2, D], BF16)
            for part in range(2):
                if loaded_by_halves(pair):
                    nc.sync.dma_start(
                        out=raw[pair][:, part, :].rearrange("p (t k) -> p t k", t=2),
                        in_=x_rows[b][:, 2 * q : 2 * q + 2, D // 2 * part : D // 2 * (part + 1)],
                    )
                else:
                    nc.sync.dma_start(out=raw[pair][:, part, :], in_=x_rows[b][:, 2 * q + part, :])

        def unit_words(unit):
            pair, half = divmod(unit, 2)
            words = raw[pair][:].rearrange("p a k -> p (a k)").bitcast(F32)
            layout = "p (h t w) -> p h t w" if loaded_by_halves(pair) else "p (t h w) -> p h t w"
            return words.rearrange(layout, h=2, t=2)[:, half, :, :]

        def sorted_in(unit):
            return min(UNIT_PASSES, SORTED_PASSES - UNIT_PASSES * (unit % 2))

        def sort_words(unit):
            ordered[unit] = stream.tile([P, 2, 2, sorted_in(unit), P], F32, name="ordered", tag="ordered", bufs=3)
            nc.vector.tensor_copy(
                out=ordered[unit][:].rearrange("p t u g (b r) -> p t u (g b) r", r=8),
                in_=unit_words(unit).rearrange("p t (a u r) -> p t u a r", u=2, r=8)[:, :, :, 0 : BLOCKS * sorted_in(unit), :],
            )

        def transpose_unit(unit):
            grouped[unit] = stream.tile([P, 4096], BF16, name="grouped", tag="grouped", bufs=4, align_bytes=64)
            for g in range(UNIT_PASSES):
                sources = [
                    ordered[unit][:, t, u, g, :]
                    if g < sorted_in(unit)
                    else every_second_word(unit_words(unit)[:, t, :], PASS_WORDS * g, u)
                    for t in range(2)
                    for u in range(2)
                ]
                transpose_bank(sources, grouped[unit][:].bitcast(F32)[:, 512 * g : 512 * (g + 1)])

        def quantize(unit, first_pass, passes):
            if first_pass == 0:
                x_codes[unit] = stream.tile([P, 1024], U32, name="x_codes", tag="x_codes", bufs=4, align_bytes=64)
                x_scales[unit] = stream.tile([P, 1024], U8, name="x_scales", tag="x_scales", bufs=4, align_bytes=64)
            columns = slice(256 * first_pass, 256 * (first_pass + passes))
            nc.vector.quantize_mx(
                out=x_codes[unit][:, columns].bitcast(E5M2X4),
                scales=x_scales[unit][:, columns],
                in_=grouped[unit][:, 4 * columns.start : 4 * columns.stop],
            )

        def multiply_unit(unit):
            for n in range(UNIT_PASSES * unit, UNIT_PASSES * (unit + 1)):
                multiply_pass(n)

        def multiply_pass(n):
            pair, g = divmod(n, PASSES)
            if g == 0:
                gates[pair] = psum.tile([P, 2 * P], F32, name="gates", tag="gates", bufs=2)
            unit = n // UNIT_PASSES
            tokens = slice(256 * (n % UNIT_PASSES), 256 * (n % UNIT_PASSES + 1))
            experts = slice(E * g, E * (g + 1))
            nc.tensor.matmul_mx(
                out=gates[pair][:],
                lhsT=w_codes[:, experts].bitcast(E4M3X4),
                lhsT_scale=w_scales[:, experts],
                rhs=x_codes[unit][:, tokens].bitcast(E5M2X4),
                rhs_scale=x_scales[unit][:, tokens],
                start=(g == 0),
                stop=(g == PASSES - 1),
            )

        def pair_view(tiles, pair):
            b, q = divmod(pair, PAIRS)
            return tiles[b][:, 2 * q : 2 * q + 2, :].rearrange("p t n -> p (t n)")

        def clamp(pair):
            b, q = divmod(pair, PAIRS)
            nc.vector.tensor_scalar(
                out=pair_view(k32, pair),
                in0=gates[pair][:],
                scalar1=EPS,
                scalar2=col_sums[b][:, q - 1 : q] if q > 0 else None,
                op0=ALU.max,
                op1=ALU.add,
                accum_out=col_sums[b][:, q : q + 1],
            )

        def split_hi(pair):
            nc.scalar.copy(out=pair_view(a_hi, pair), in_=pair_view(k32, pair))

        def split_lo(pair):
            nc.vector.tensor_tensor(
                out=pair_view(a_lo, pair), in0=pair_view(k32, pair), in1=pair_view(a_hi, pair), op=ALU.subtract
            )

        def transpose_terms(pair):
            b, q = divmod(pair, PAIRS)
            bank = bank_tile([P, 2, 2, P], BF16)
            for t in range(2):
                nc.tensor.transpose(bank[:, t, 0, :], a_hi[b][:, 2 * q + t, :], ident16[:])
                nc.tensor.transpose(bank[:, t, 1, :], a_lo[b][:, 2 * q + t, :], ident16[:])
            nc.scalar.copy(out=b_terms[b][:, 2 * q : 2 * q + 2, :, :], in_=bank[:])

        def invert_leading(b, h):
            width = TILES if h % 2 == 0 else 1
            factors[b, h] = small.tile([P, width], F32, name="factors", tag="factors", bufs=8)
            terms[b, h] = small.tile([P, 2, TILES], BF16, name="terms", tag="terms", bufs=8)
            totals[b, h] = small.tile([P, width], F32, name="totals", tag="totals", bufs=8)
            if h < 0:
                nc.vector.tensor_scalar(
                    out=totals[b, h][:], in0=col_sums[b][:, PAIRS - 1 : PAIRS], scalar1=FIRST_SCALE, scalar2=None, op0=ALU.mult
                )
                nc.vector.reciprocal(out=terms[b, h][:, 0, 0:width], in_=totals[b, h][:])
            else:
                nc.vector.reciprocal(out=terms[b, h][:, 0, 0:width], in_=sums[b, h][:, :, 0])
                nc.vector.tensor_reduce(out=totals[b, h][:], in_=sums[b, h][:, :, 0:3], axis=AX.X, op=ALU.add)

        def invert_total(b, h):
            nc.vector.reciprocal(out=factors[b, h][:], in_=totals[b, h][:])

        def invert_remainder(b, h):
            width = TILES if h % 2 == 0 else 1
            nc.vector.tensor_tensor(
                out=terms[b, h][:, 1, 0:width], in0=factors[b, h][:], in1=terms[b, h][:, 0, 0:width], op=ALU.subtract
            )

        def invert(b, h):
            invert_leading(b, h)
            invert_total(b, h)
            invert_remainder(b, h)

        def sum_part(b, h, part):
            is_row_step = h % 2 == 0
            if part == 0:
                shape = [P, TILES if is_row_step else 1, 4]
                sums[b, h] = psum.tile(shape, F32, name="sums", tag="sums", bufs=1) if b == 0 else bank_tile(shape, F32)
            out_columns = slice(2, 3) if part == 0 else slice(0, 2)
            used_terms = slice(0, 1) if part == 0 else slice(0, 2)
            for j in range(TILES):
                if is_row_step:
                    nc.tensor.matmul(
                        sums[b, h][:, j, out_columns],
                        lhsT=(a_lo if part == 0 else a_hi)[b][:, j, :],
                        rhs=terms[b, h - 1][:, used_terms, 0],
                        start=True,
                        stop=True,
                    )
                else:
                    nc.tensor.matmul(
                        sums[b, h][:, 0, out_columns],
                        lhsT=b_terms[b][:, j, 1 - part, :],
                        rhs=terms[b, h - 1][:, used_terms, j],
                        start=(j == 0),
                        stop=(j == TILES - 1),
                    )

        def scale_columns(b, quarters_on_vector):
            column = factors[b, HALF_STEPS - 2][:]
            scaled[b] = wide_tile([P, TILES, P], F32)
            results[b] = wide_tile([P, TILES, P], F32)
            for quarter in range(4):
                tiles = slice(4 * quarter, 4 * quarter + 4)
                if quarter < quarters_on_vector:
                    nc.vector.tensor_scalar(
                        out=scaled[b][:, tiles, :], in0=k32[b][:, tiles, :], scalar1=column, scalar2=None, op0=ALU.mult
                    )
                else:
                    nc.scalar.activation(out=scaled[b][:, tiles, :], in_=k32[b][:, tiles, :], func=ACT.Copy, scale=column)

        def finish_quarter(b, quarter, on_vector):
            row = factors[b, HALF_STEPS - 1]
            tiles = slice(4 * quarter, 4 * quarter + 4)
            bank = bank_tile([P, 4, P], F32)
            for t in range(4):
                nc.tensor.transpose(bank[:, t, :], scaled[b][:, 4 * quarter + t, :], ident32[:])
            if on_vector:
                nc.vector.tensor_tensor(
                    out=results[b][:, tiles, :],
                    in0=bank[:],
                    in1=row[:, tiles].unsqueeze(2).to_broadcast([P, 4, P]),
                    op=ALU.mult,
                )
            else:
                for t in range(4):
                    j = 4 * quarter + t
                    nc.scalar.activation(out=results[b][:, j, :], in_=bank[:, t, :], func=ACT.Copy, scale=row[:, j : j + 1])
            nc.sync.dma_start(out=out_rows[b][:, tiles, :], in_=results[b][:, tiles, :])

        w_grouped = prepare_w()
        for pair in range(LOAD_AHEAD):
            load(pair)
        for unit in range(SORT_AHEAD):
            sort_words(unit)
        nc.vector.quantize_mx(out=w_codes[:].bitcast(E4M3X4), scales=w_scales[:], in_=w_grouped[:])

        def pair_at(unit, lag):
            pair, odd = divmod(unit - lag, 2)
            return pair if odd == 0 and pair >= 0 else None

        first_woven_unit = 2 * (PAIRS - 1) + 6
        for unit in range(UNITS):
            woven = unit - first_woven_unit
            inverting = woven // 2 - 1 if woven >= 0 and woven % 2 == 0 else None
            if unit % 2 == 0 and unit // 2 + LOAD_AHEAD < B * PAIRS:
                load(unit // 2 + LOAD_AHEAD)
            if unit + SORT_AHEAD < UNITS:
                sort_words(unit + SORT_AHEAD)
            if inverting is not None:
                invert_leading(0, inverting)
            if unit >= 1:
                quantize(unit - 1, 0, UNIT_PASSES)
            if inverting is not None:
                invert_total(0, inverting)
            if pair_at(unit, 4) is not None:
                clamp(pair_at(unit, 4))
            if pair_at(unit, 5) is not None:
                split_lo(pair_at(unit, 5))
            if inverting is not None:
                invert_remainder(0, inverting)
            transpose_unit(unit)
            if pair_at(unit, 6) is not None:
                transpose_terms(pair_at(unit, 6))
            if woven >= 0:
                sum_part(0, woven // 2, woven % 2)
            if unit >= 2:
                multiply_unit(unit - 2)
            if pair_at(unit, 4) is not None:
                split_hi(pair_at(unit, 4))

        last = B * PAIRS - 1
        step0 = (UNITS - first_woven_unit) // 2
        invert(0, step0 - 1)
        clamp(last - 1)
        transpose_terms(last - 2)
        multiply_unit(UNITS - 2)
        sum_part(0, step0, 0)
        sum_part(0, step0, 1)
        quantize(UNITS - 1, 0, 2)
        split_hi(last - 1)
        quantize(UNITS - 1, 2, 2)
        multiply_unit(UNITS - 1)
        invert_leading(0, step0)
        split_lo(last - 1)
        invert_total(0, step0)
        invert_remainder(0, step0)
        transpose_terms(last - 1)
        sum_part(0, step0 + 1, 0)
        sum_part(0, step0 + 1, 1)
        clamp(last)
        split_hi(last)
        invert_leading(1, -1)
        split_lo(last)
        invert_total(1, -1)
        invert_remainder(1, -1)
        invert(0, step0 + 1)

        parts_left = [(h, part) for h in range(step0 + 2, HALF_STEPS) for part in range(2)]
        part_gaps = HALF_STEPS - 1 - 4
        double_gaps = len(parts_left) - part_gaps
        for h in range(HALF_STEPS):
            sum_part(1, h, 0)
            sum_part(1, h, 1)
            if h == 0:
                transpose_terms(last)
            invert(1, h)
            if h == HALF_STEPS - 2:
                scale_columns(1, 2)
            if h < part_gaps:
                for h0, part in parts_left[h + min(h, double_gaps) : h + 1 + min(h + 1, double_gaps)]:
                    sum_part(0, h0, part)
                    if part == 1:
                        invert(0, h0)
                        if h0 == HALF_STEPS - 2:
                            scale_columns(0, 0)
            elif h < HALF_STEPS - 1:
                finish_quarter(0, h - part_gaps, False)
        for quarter in range(4):
            finish_quarter(1, quarter, quarter % 2 == 1)
